import numpy as np
import ml_dtypes


def mxq(x, axis, fmt="e4m3"):
    dtype, down = {"e4m3": (ml_dtypes.float8_e4m3fn, 7), "e5m2": (ml_dtypes.float8_e5m2, 14)}[fmt]
    v = np.moveaxis(np.asarray(x, np.float32).astype(ml_dtypes.bfloat16).astype(np.float64), axis, -1)
    blocks = v.reshape(v.shape[:-1] + (-1, 32))
    amax = np.abs(blocks).max(-1, keepdims=True)
    byte = np.maximum(np.where(amax > 0, np.frexp(amax)[1] - 1 + 127, 0) - down, 1)
    scale = np.exp2(byte - 127.0)
    codes = (blocks / scale).astype(np.float32).astype(dtype).astype(np.float64)
    return np.moveaxis((codes * scale).reshape(v.shape), -1, axis)


WIDE = False


def mx_kscale(k):
    if not WIDE:
        return np.ones(k)
    levels = np.array([10, -10, 5, -5, 0])
    a = np.random.permutation(np.resize(levels, k // 512 * 4)).reshape(k // 512, 4)
    idx = np.arange(k)
    return np.exp2(a[idx // 512, idx % 128 // 32])


BF16 = ml_dtypes.bfloat16


def bf(x):
    return np.asarray(x, np.float32).astype(BF16)


def f64(x):
    return np.asarray(x).astype(np.float64)


E2M1 = np.array([0.0, 0.5, 1.0, 1.5, 2.0, 3.0, 4.0, 6.0, -0.0, -0.5, -1.0, -1.5, -2.0, -3.0, -4.0, -6.0])


def pack_weight(w, fmt):
    k, n = w.shape
    w = f64(bf(w)).reshape(k // 32, 32, n)
    amax = np.abs(w).max(1)
    if fmt == "e4m3":
        byte = np.frexp(amax)[1] - 1 + 127 - 7
    else:
        mant, ex = np.frexp(amax / 6.0)
        byte = np.where(mant > 0.5, ex, ex - 1) + 127
    byte = np.clip(np.where(amax > 0, byte, 1), 1, 254)
    scaled = (w * np.exp2(127.0 - byte)[:, None, :]).reshape(k, n).astype(np.float32)
    by_word = np.ascontiguousarray(scaled.reshape(k // 512, 128, 4, n).transpose(0, 1, 3, 2))
    if fmt == "e4m3":
        words = by_word.astype(ml_dtypes.float8_e4m3fn).view(np.uint8)
    else:
        c = by_word.astype(ml_dtypes.float4_e2m1fn).view(np.uint8) & 0xF
        words = c[..., 0::2] | (c[..., 1::2] << 4)
    return np.ascontiguousarray(words), np.ascontiguousarray(byte.astype(np.uint8).reshape(k // 512, 16, n))


def unpack_weight(words, scales, fmt):
    g, p, n, _ = words.shape
    if fmt == "e4m3":
        vals = np.ascontiguousarray(words).view(ml_dtypes.float8_e4m3fn).astype(np.float64)
    else:
        nib = np.empty((g, p, n, 4), np.uint8)
        nib[..., 0::2] = words & 0xF
        nib[..., 1::2] = words >> 4
        vals = E2M1[nib]
    vals = vals * np.repeat(np.exp2(scales.astype(np.float64) - 127.0), 8, axis=1)[..., None]
    return vals.transpose(0, 1, 3, 2).reshape(g * 512, n)


B, D, H, G, L, P = 256, 1024, 1024, 4, 4, 2
FMT = "e4m3"


def sigmoid(v):
    return 1.0 / (1.0 + np.exp(-v))


def setup_inputs():
    s, u = mx_kscale(H), mx_kscale(H)
    w_ih = np.random.standard_normal((G, P, H, H)) * 1.5 / np.sqrt(H)
    w_ih[:, 0] = w_ih[:, 0] / s[:, None]
    w_hh = np.random.standard_normal((G, P, H, H)) / np.sqrt(H) / u[:, None]
    w_ih_words, w_ih_scales = pack_weight(w_ih.reshape(-1, H), FMT)
    w_hh_words, w_hh_scales = pack_weight(w_hh.reshape(-1, H), FMT)
    return {"x": bf(np.random.standard_normal((B, H)) * s),
            "hidden": bf(np.random.standard_normal((B, H)) * u),
            "cell_state": bf(np.random.standard_normal((B, H))),
            "w_ih_words": w_ih_words,
            "w_ih_scales": w_ih_scales,
            "w_hh_words": w_hh_words,
            "w_hh_scales": w_hh_scales,
            "b_ih": bf(np.random.standard_normal((G, P, H)) * 0.3),
            "b_hh": bf(np.random.standard_normal((G, P, H)) * 0.3)}


def reference(x, hidden, cell_state, w_ih_words, w_ih_scales, w_hh_words, w_hh_scales, b_ih, b_hh):
    x, c = f64(x), f64(cell_state)
    b_ih, b_hh = f64(b_ih), f64(b_hh)
    w_ih = unpack_weight(w_ih_words, w_ih_scales, FMT).reshape(G, P, H, H)
    w_hh = unpack_weight(w_hh_words, w_hh_scales, FMT).reshape(G, P, H, H)
    hq = mxq(f64(hidden), 1, "e4m3")
    for l in range(P):
        gates = ((mxq(x, 1, "e4m3") @ w_ih[:, l])
                 + (hq @ w_hh[:, l])
                 + b_ih[:, l][:, None, :] + b_hh[:, l][:, None, :])
        z_i, z_f, z_g, z_o = gates
        i_t = sigmoid(z_i)
        f_t = sigmoid(z_f)
        g_t = np.tanh(z_g)
        o_t = sigmoid(z_o)
        c = f_t * c + i_t * g_t
        x = o_t * np.tanh(c)
    return x, c

@@ -1,0 +1,267 @@
+from contextlib import ExitStack
+
+import concourse.mybir as mybir
+from concourse.masks import make_identity
+
+F32 = mybir.dt.float32
+BF16 = mybir.dt.bfloat16
+I32 = mybir.dt.int32
+U32 = mybir.dt.uint32
+U8 = mybir.dt.uint8
+FP8X4 = mybir.dt.float8_e4m3fn_x4
+SIGMOID = mybir.ActivationFunctionType.Sigmoid
+TANH = mybir.ActivationFunctionType.Tanh
+ADD = mybir.AluOpType.add
+MULT = mybir.AluOpType.mult
+
+P = 128
+PACK = 4
+BATCH = 256
+HIDDEN = 1024
+LAYERS = 2
+GATES = 4
+BATCH_TILES = BATCH // P
+K_PASSES = HIDDEN // (P * PACK)
+HALF = 512
+HALVES = HIDDEN // HALF
+
+GATE_I = 0
+GATE_F = 1
+GATE_G = 2
+GATE_O = 3
+GATE_ORDER = (GATE_F, GATE_I, GATE_G, GATE_O)
+GATE_FUNC = {GATE_I: SIGMOID, GATE_F: SIGMOID, GATE_G: TANH, GATE_O: SIGMOID}
+
+HH = 0
+IH = 1
+
+FLOPS = 2 * LAYERS * GATES * 2 * BATCH * HIDDEN * HIDDEN
+
+
+def tile_lstm_pa_e_kernel(
+    tc, x, hidden, cell_state, w_ih_words, w_ih_scales, w_hh_words, w_hh_scales, b_ih, b_hh, out_0, out_1
+):
+    nc = tc.nc
+    words_in_hbm = {HH: w_hh_words, IH: w_ih_words}
+    scales_in_hbm = {HH: w_hh_scales, IH: w_ih_scales}
+    pieces = [(h, j) for h in range(HALVES) for j in range(BATCH_TILES)]
+
+    def by_partition(array):
+        return array.rearrange("(p j) n -> p j n", j=BATCH_TILES)
+
+    def columns(h):
+        return slice(h * HALF, (h + 1) * HALF)
+
+    with ExitStack() as stack:
+        stack.enter_context(tc.manual_schedule())
+        keep = stack.enter_context(tc.tile_pool(name="keep", bufs=1))
+        weight_pool = stack.enter_context(tc.tile_pool(name="weights", bufs=GATES * 2 * K_PASSES))
+        stage = stack.enter_context(tc.tile_pool(name="stage", bufs=2))
+        work = stack.enter_context(tc.tile_pool(name="work", bufs=1))
+        sums = stack.enter_context(tc.psum_pool(name="sums", bufs=6))
+        flips = stack.enter_context(tc.psum_pool(name="flips", bufs=2))
+
+        planes = keep.tile([P, LAYERS * 2 * K_PASSES, HIDDEN], U8, align_bytes=64)
+        nc.vector.memset(planes[:].rearrange("p s n -> p (s n)").bitcast(I32), 0)
+
+        def slab(layer, kind, g):
+            return (layer * 2 + kind) * K_PASSES + g
+
+        bias_rows = keep.tile([P, HALF], BF16)
+        nc.vector.memset(bias_rows[:], 0.0)
+        n_bias_rows = GATES * LAYERS * HALVES
+        nc.scalar.dma_start(out=bias_rows[0:n_bias_rows, :], in_=b_ih.rearrange("k l (h n) -> (k l h) n", h=HALVES))
+        nc.scalar.dma_start(
+            out=bias_rows[n_bias_rows : 2 * n_bias_rows, :], in_=b_hh.rearrange("k l (h n) -> (k l h) n", h=HALVES)
+        )
+
+        table_warmer = keep.tile([P, 1], F32)
+        nc.vector.memset(table_warmer[:], 0.0)
+        nc.scalar.activation(out=table_warmer[:], in_=table_warmer[:], func=SIGMOID)
+
+        ident_bf16 = keep.tile([P, P], BF16)
+        make_identity(nc, ident_bf16[:])
+        ident_f32 = keep.tile([P, P], F32)
+        make_identity(nc, ident_f32[:])
+        bias_pick = keep.tile([P, n_bias_rows], BF16)
+        nc.vector.tensor_tensor(
+            out=bias_pick[:],
+            in0=ident_bf16[:, 0:n_bias_rows],
+            in1=ident_bf16[:, n_bias_rows : 2 * n_bias_rows],
+            op=ADD,
+        )
+
+        hidden_sb = keep.tile([P, BATCH_TILES, HIDDEN], BF16)
+        nc.sync.dma_start(out=hidden_sb[:], in_=by_partition(hidden))
+        x_sb = keep.tile([P, BATCH_TILES, HIDDEN], BF16)
+        nc.sync.dma_start(out=x_sb[:], in_=by_partition(x))
+        cell_sb = keep.tile([P, BATCH_TILES, HIDDEN], BF16)
+
+        def load_scale_planes(layer):
+            for kind in (HH, IH):
+                by_gate = scales_in_hbm[kind].rearrange("(k l g) q n -> l g k q n", k=GATES, l=LAYERS)
+                for g in range(K_PASSES):
+                    for quadrant in range(4):
+                        nc.sync.dma_start(
+                            out=planes[32 * quadrant : 32 * quadrant + 16, slab(layer, kind, g), :].bitcast(I32),
+                            in_=by_gate[layer, g, :, 4 * quadrant : 4 * quadrant + 4, :].bitcast(I32),
+                        )
+
+        weights = {}
+
+        def load_gate_weights(layer, gate):
+            for kind in (HH, IH):
+                for g in range(K_PASSES):
+                    w = weight_pool.tile([P, HIDDEN], I32, name="w", tag="w", align_bytes=64)
+                    group = (gate * LAYERS + layer) * K_PASSES + g
+                    nc.sync.dma_start(out=w[:], in_=words_in_hbm[kind][group].rearrange("p n t -> p (n t)").bitcast(I32))
+                    weights[(layer, gate, kind, g)] = w
+
+        load_scale_planes(0)
+        for gate in GATE_ORDER:
+            load_gate_weights(0, gate)
+            if gate == GATE_ORDER[0]:
+                nc.sync.dma_start(out=cell_sb[:], in_=by_partition(cell_state))
+
+        bias_all = keep.tile([P, n_bias_rows, HALF], F32)
+
+        def bias_row(layer, gate, h):
+            return (gate * LAYERS + layer) * HALVES + h
+
+        def spread_bias(layer):
+            for gate in GATE_ORDER:
+                for h in range(HALVES):
+                    r = bias_row(layer, gate, h)
+                    bias_bank = sums.tile([P, HALF], F32, tag="sum")
+                    nc.tensor.matmul(
+                        out=bias_bank[:],
+                        lhsT=bias_pick[:, r : r + 1].to_broadcast([P, P]),
+                        rhs=bias_rows[:],
+                        start=True,
+                        stop=True,
+                    )
+                    if h == 0:
+                        nc.scalar.copy(out=bias_all[:, r, :], in_=bias_bank[:])
+                    else:
+                        nc.vector.tensor_copy(out=bias_all[:, r, :], in_=bias_bank[:])
+
+        def new_mx_operand(name):
+            codes = keep.tile([P, BATCH_TILES, K_PASSES, P], U32, name=name + "_codes", align_bytes=64)
+            scales = keep.tile([P, BATCH_TILES, K_PASSES, P], U8, name=name + "_scales", align_bytes=64)
+            return codes, scales
+
+        def quantise_input(source_sb, codes, scales):
+            for j in range(BATCH_TILES):
+                pairs = source_sb[:, j, :].bitcast(F32)
+                flipped = flips.tile([P, K_PASSES, 2, P], F32, tag="flip")
+                for g in range(K_PASSES):
+                    for u in range(2):
+                        first = (HALF // 2) * g + u
+                        nc.tensor.transpose(flipped[:, g, u, :], pairs[:, first : (HALF // 2) * (g + 1) : 2], ident_f32[:])
+                grouped = stage.tile([P, K_PASSES * P * PACK], BF16, tag="grouped", align_bytes=64)
+                nc.scalar.copy(
+                    out=grouped[:].bitcast(F32).rearrange("p (g b u) -> p g b u", g=K_PASSES, u=2),
+                    in_=flipped[:].rearrange("p g u b -> p g b u"),
+                )
+                nc.vector.quantize_mx(
+                    out=codes[:, j].rearrange("p g b -> p (g b)").bitcast(FP8X4),
+                    scales=scales[:, j].rearrange("p g b -> p (g b)"),
+                    in_=grouped[:],
+                )
+
+        hidden_codes, hidden_scales = new_mx_operand("hidden")
+        x_codes, x_scales = new_mx_operand("x")
+        x1_codes, x1_scales = new_mx_operand("x1")
+        layer_input = {0: (x_codes, x_scales), 1: (x1_codes, x1_scales)}
+
+        spread_bias(0)
+        quantise_input(hidden_sb, hidden_codes, hidden_scales)
+        quantise_input(x_sb, x_codes, x_scales)
+        spread_bias(1)
+
+        def mx_passes(banks, layer, gate, kind, codes, scales):
+            for g in range(K_PASSES):
+                w = weights[(layer, gate, kind, g)]
+                for h, j in pieces:
+                    nc.tensor.matmul_mx(
+                        out=banks[(h, j)][:],
+                        lhsT=codes[:, j, g, :].bitcast(FP8X4),
+                        lhsT_scale=scales[:, j, g, :],
+                        rhs=w[:, columns(h)].bitcast(FP8X4),
+                        rhs_scale=planes[4 * gate : P, slab(layer, kind, g), columns(h)],
+                        start=(kind == HH and g == 0),
+                        stop=(kind == IH and g == K_PASSES - 1),
+                    )
+
+        def open_gate(layer, gate):
+            banks = {}
+            for h, j in pieces:
+                banks[(h, j)] = sums.tile([P, HALF], F32, name="gate_bank", tag="sum")
+            mx_passes(banks, layer, gate, HH, hidden_codes, hidden_scales)
+            return banks
+
+        def on_pieces(tile):
+            return [tile[:, j, columns(h)] for h, j in pieces]
+
+        steps = [(layer, gate) for layer in range(LAYERS) for gate in GATE_ORDER]
+        cell = {0: cell_sb}
+        acts = {}
+        x1_sb = keep.tile([P, BATCH_TILES, HIDDEN], BF16)
+
+        banks = open_gate(*steps[0])
+        for n, (layer, gate) in enumerate(steps):
+            mx_passes(banks, layer, gate, IH, *layer_input[layer])
+            if layer == 0:
+                if gate == GATE_ORDER[0]:
+                    load_scale_planes(1)
+                load_gate_weights(1, gate)
+
+            act = work.tile([P, BATCH_TILES, HIDDEN], F32, name="act%d" % gate, tag="act%d" % gate)
+            acts[gate] = act
+            for h, j in pieces:
+                nc.vector.tensor_tensor(
+                    out=act[:, j, columns(h)], in0=banks[(h, j)][:], in1=bias_all[:, bias_row(layer, gate, h), :], op=ADD
+                )
+            if n + 1 < len(steps):
+                banks = open_gate(*steps[n + 1])
+
+            for piece in on_pieces(act):
+                nc.scalar.activation(out=piece, in_=piece, func=GATE_FUNC[gate])
+
+            if gate == GATE_F:
+                for f, c in zip(on_pieces(act), on_pieces(cell[layer])):
+                    nc.vector.tensor_tensor(out=f, in0=f, in1=c, op=MULT)
+            if gate == GATE_G:
+                new_cell = work.tile([P, BATCH_TILES, HIDDEN], F32, name="cell", tag="cell", bufs=2)
+                cell[layer + 1] = new_cell
+                tanh_cell = work.tile([P, BATCH_TILES, HIDDEN], F32, name="tanh_cell", tag="tanh_cell")
+                for i, g_act in zip(on_pieces(acts[GATE_I]), on_pieces(act)):
+                    nc.vector.tensor_tensor(out=i, in0=i, in1=g_act, op=MULT)
+                for c, fc, ig in zip(on_pieces(new_cell), on_pieces(acts[GATE_F]), on_pieces(acts[GATE_I])):
+                    nc.vector.tensor_tensor(out=c, in0=fc, in1=ig, op=ADD)
+                for t, c in zip(on_pieces(tanh_cell), on_pieces(new_cell)):
+                    nc.scalar.activation(out=t, in_=c, func=TANH)
+                if layer == LAYERS - 1:
+                    for c_hbm, c in zip(on_pieces(by_partition(out_1)), on_pieces(new_cell)):
+                        nc.sync.dma_start(out=c_hbm, in_=c)
+            if gate == GATE_O and layer == 0:
+                for x1, o, t in zip(on_pieces(x1_sb), on_pieces(act), on_pieces(tanh_cell)):
+                    nc.vector.tensor_tensor(out=x1, in0=o, in1=t, op=MULT)
+                grouped_x1 = {}
+                for g, j in pieces:
+                    flipped = flips.tile([P, PACK, P], BF16, tag="flip")
+                    for t in range(PACK):
+                        nc.tensor.transpose(flipped[:, t, :], x1_sb[:, j, HALF * g + t : HALF * (g + 1) : PACK], ident_bf16[:])
+                    grouped = stage.tile([P, P, PACK], BF16, tag="grouped_x1", bufs=len(pieces), align_bytes=64)
+                    nc.scalar.copy(out=grouped[:], in_=flipped[:].rearrange("p t b -> p b t"))
+                    grouped_x1[(g, j)] = grouped
+                for g, j in pieces:
+                    nc.vector.quantize_mx(
+                        out=x1_codes[:, j, g, :].bitcast(FP8X4),
+                        scales=x1_scales[:, j, g, :],
+                        in_=grouped_x1[(g, j)][:].rearrange("p b t -> p (b t)"),
+                    )
+            if gate == GATE_O and layer == LAYERS - 1:
+                for x2_hbm, o, t in zip(on_pieces(by_partition(out_0)), on_pieces(act), on_pieces(tanh_cell)):
+                    nc.vector.tensor_tensor(out=o, in0=o, in1=t, op=MULT)
+                    nc.sync.dma_start(out=x2_hbm, in_=o)

@@ -55,34 +55,30 @@ def tile_lstm_pa_e_kernel(
     with ExitStack() as stack:
         stack.enter_context(tc.manual_schedule())
         keep = stack.enter_context(tc.tile_pool(name="keep", bufs=1))
-        weight_pool = stack.enter_context(tc.tile_pool(name="weights", bufs=GATES * 2 * K_PASSES))
+        weight_pool = stack.enter_context(tc.tile_pool(name="weights", bufs=12))
         stage = stack.enter_context(tc.tile_pool(name="stage", bufs=2))
         work = stack.enter_context(tc.tile_pool(name="work", bufs=1))
         sums = stack.enter_context(tc.psum_pool(name="sums", bufs=6))
         flips = stack.enter_context(tc.psum_pool(name="flips", bufs=2))
 
-        planes = keep.tile([P, LAYERS * 2 * K_PASSES, HIDDEN], U8, align_bytes=64)
-        nc.vector.memset(planes[:].rearrange("p s n -> p (s n)").bitcast(I32), 0)
-
-        def slab(layer, kind, g):
-            return (layer * 2 + kind) * K_PASSES + g
-
         bias_rows = keep.tile([P, HALF], BF16)
-        nc.vector.memset(bias_rows[:], 0.0)
         n_bias_rows = GATES * LAYERS * HALVES
+        nc.gpsimd.memset(bias_rows[:], 0.0)
         nc.scalar.dma_start(out=bias_rows[0:n_bias_rows, :], in_=b_ih.rearrange("k l (h n) -> (k l h) n", h=HALVES))
         nc.scalar.dma_start(
             out=bias_rows[n_bias_rows : 2 * n_bias_rows, :], in_=b_hh.rearrange("k l (h n) -> (k l h) n", h=HALVES)
         )
 
-        table_warmer = keep.tile([P, 1], F32)
-        nc.vector.memset(table_warmer[:], 0.0)
-        nc.scalar.activation(out=table_warmer[:], in_=table_warmer[:], func=SIGMOID)
+        planes = {}
+        for gate in GATE_ORDER:
+            for kind in (HH, IH):
+                planes[(gate, kind)] = keep.tile([P, HIDDEN], U8, name="planes%d%d" % (gate, kind), align_bytes=64)
+                nc.vector.memset(planes[(gate, kind)][:].bitcast(I32), 0)
 
-        ident_bf16 = keep.tile([P, P], BF16)
-        make_identity(nc, ident_bf16[:])
         ident_f32 = keep.tile([P, P], F32)
         make_identity(nc, ident_f32[:])
+        ident_bf16 = keep.tile([P, P], BF16)
+        make_identity(nc, ident_bf16[:])
         bias_pick = keep.tile([P, n_bias_rows], BF16)
         nc.vector.tensor_tensor(
             out=bias_pick[:],
@@ -90,36 +86,38 @@ def tile_lstm_pa_e_kernel(
             in1=ident_bf16[:, n_bias_rows : 2 * n_bias_rows],
             op=ADD,
         )
+        table_warmer = keep.tile([P, 1], F32)
+        nc.vector.memset(table_warmer[:], 0.0)
+        nc.scalar.activation(out=table_warmer[:], in_=table_warmer[:], func=SIGMOID)
 
         hidden_sb = keep.tile([P, BATCH_TILES, HIDDEN], BF16)
-        nc.sync.dma_start(out=hidden_sb[:], in_=by_partition(hidden))
         x_sb = keep.tile([P, BATCH_TILES, HIDDEN], BF16)
-        nc.sync.dma_start(out=x_sb[:], in_=by_partition(x))
         cell_sb = keep.tile([P, BATCH_TILES, HIDDEN], BF16)
 
-        def load_scale_planes(layer):
-            for kind in (HH, IH):
-                by_gate = scales_in_hbm[kind].rearrange("(k l g) q n -> l g k q n", k=GATES, l=LAYERS)
-                for g in range(K_PASSES):
-                    for quadrant in range(4):
-                        nc.sync.dma_start(
-                            out=planes[32 * quadrant : 32 * quadrant + 16, slab(layer, kind, g), :].bitcast(I32),
-                            in_=by_gate[layer, g, :, 4 * quadrant : 4 * quadrant + 4, :].bitcast(I32),
-                        )
+        def load_scale_planes(gate, kind):
+            by_plane = scales_in_hbm[kind].rearrange("(k s) q n -> k s q n", k=GATES)
+            for quadrant in range(4):
+                nc.sync.dma_start(
+                    out=planes[(gate, kind)][32 * quadrant : 32 * quadrant + 16, :].bitcast(I32),
+                    in_=by_plane[gate, :, 4 * quadrant : 4 * quadrant + 4, :].bitcast(I32),
+                )
 
         weights = {}
 
-        def load_gate_weights(layer, gate):
-            for kind in (HH, IH):
-                for g in range(K_PASSES):
-                    w = weight_pool.tile([P, HIDDEN], I32, name="w", tag="w", align_bytes=64)
-                    group = (gate * LAYERS + layer) * K_PASSES + g
-                    nc.sync.dma_start(out=w[:], in_=words_in_hbm[kind][group].rearrange("p n t -> p (n t)").bitcast(I32))
-                    weights[(layer, gate, kind, g)] = w
+        def load_weights(layer, gate, kind):
+            w = weight_pool.tile([P, K_PASSES, HIDDEN], I32, name="w", tag="w", align_bytes=64)
+            first = (gate * LAYERS + layer) * K_PASSES
+            source = words_in_hbm[kind][first : first + K_PASSES].rearrange("g p n t -> p g (n t)").bitcast(I32)
+            nc.sync.dma_start(out=w[:], in_=source)
+            weights[(layer, gate, kind)] = w
 
-        load_scale_planes(0)
+        nc.sync.dma_start(out=hidden_sb[:], in_=by_partition(hidden))
         for gate in GATE_ORDER:
-            load_gate_weights(0, gate)
+            for kind in (HH, IH):
+                load_scale_planes(gate, kind)
+                load_weights(0, gate, kind)
+                if gate == GATE_ORDER[0] and kind == HH:
+                    nc.sync.dma_start(out=x_sb[:], in_=by_partition(x))
             if gate == GATE_ORDER[0]:
                 nc.sync.dma_start(out=cell_sb[:], in_=by_partition(cell_state))
 
@@ -174,21 +172,22 @@ def tile_lstm_pa_e_kernel(
         x1_codes, x1_scales = new_mx_operand("x1")
         layer_input = {0: (x_codes, x_scales), 1: (x1_codes, x1_scales)}
 
-        spread_bias(0)
         quantise_input(hidden_sb, hidden_codes, hidden_scales)
+        spread_bias(0)
         quantise_input(x_sb, x_codes, x_scales)
         spread_bias(1)
 
         def mx_passes(banks, layer, gate, kind, codes, scales):
             for g in range(K_PASSES):
-                w = weights[(layer, gate, kind, g)]
+                w = weights[(layer, gate, kind)]
+                plane = 4 * (layer * K_PASSES + g)
                 for h, j in pieces:
                     nc.tensor.matmul_mx(
                         out=banks[(h, j)][:],
                         lhsT=codes[:, j, g, :].bitcast(FP8X4),
                         lhsT_scale=scales[:, j, g, :],
-                        rhs=w[:, columns(h)].bitcast(FP8X4),
-                        rhs_scale=planes[4 * gate : P, slab(layer, kind, g), columns(h)],
+                        rhs=w[:, g, columns(h)].bitcast(FP8X4),
+                        rhs_scale=planes[(gate, kind)][plane:P, columns(h)],
                         start=(kind == HH and g == 0),
                         stop=(kind == IH and g == K_PASSES - 1),
                     )
@@ -212,9 +211,8 @@ def tile_lstm_pa_e_kernel(
         for n, (layer, gate) in enumerate(steps):
             mx_passes(banks, layer, gate, IH, *layer_input[layer])
             if layer == 0:
-                if gate == GATE_ORDER[0]:
-                    load_scale_planes(1)
-                load_gate_weights(1, gate)
+                for kind in (HH, IH):
+                    load_weights(1, gate, kind)
 
             act = work.tile([P, BATCH_TILES, HIDDEN], F32, name="act%d" % gate, tag="act%d" % gate)
             acts[gate] = act

@@ -29,7 +29,20 @@ GATE_I = 0
 GATE_F = 1
 GATE_G = 2
 GATE_O = 3
-GATE_ORDER = (GATE_F, GATE_I, GATE_G, GATE_O)
+BOTH = (0, 1)
+STEPS = (
+    (0, GATE_F, BOTH),
+    (0, GATE_I, BOTH),
+    (0, GATE_G, BOTH),
+    (0, GATE_O, BOTH),
+    (1, GATE_F, BOTH),
+    (1, GATE_I, (0,)),
+    (1, GATE_G, (0,)),
+    (1, GATE_I, (1,)),
+    (1, GATE_G, (1,)),
+    (1, GATE_O, (0,)),
+    (1, GATE_O, (1,)),
+)
 GATE_FUNC = {GATE_I: SIGMOID, GATE_F: SIGMOID, GATE_G: TANH, GATE_O: SIGMOID}
 
 HH = 0
@@ -44,7 +57,6 @@ def tile_lstm_pa_e_kernel(
     nc = tc.nc
     words_in_hbm = {HH: w_hh_words, IH: w_ih_words}
     scales_in_hbm = {HH: w_hh_scales, IH: w_ih_scales}
-    pieces = [(h, j) for h in range(HALVES) for j in range(BATCH_TILES)]
 
     def by_partition(array):
         return array.rearrange("(p j) n -> p j n", j=BATCH_TILES)
@@ -55,11 +67,10 @@ def tile_lstm_pa_e_kernel(
     with ExitStack() as stack:
         stack.enter_context(tc.manual_schedule())
         keep = stack.enter_context(tc.tile_pool(name="keep", bufs=1))
-        weight_pool = stack.enter_context(tc.tile_pool(name="weights", bufs=12))
+        weight_pool = stack.enter_context(tc.tile_pool(name="weights", bufs=24))
         stage = stack.enter_context(tc.tile_pool(name="stage", bufs=2))
         work = stack.enter_context(tc.tile_pool(name="work", bufs=1))
-        sums = stack.enter_context(tc.psum_pool(name="sums", bufs=6))
-        flips = stack.enter_context(tc.psum_pool(name="flips", bufs=2))
+        psum = stack.enter_context(tc.psum_pool(name="psum", bufs=8))
 
         bias_rows = keep.tile([P, HALF], BF16)
         n_bias_rows = GATES * LAYERS * HALVES
@@ -69,11 +80,11 @@ def tile_lstm_pa_e_kernel(
             out=bias_rows[n_bias_rows : 2 * n_bias_rows, :], in_=b_hh.rearrange("k l (h n) -> (k l h) n", h=HALVES)
         )
 
+        slabs = [(layer, kind, g) for layer in range(LAYERS) for kind in (HH, IH) for g in range(K_PASSES)]
         planes = {}
-        for gate in GATE_ORDER:
-            for kind in (HH, IH):
-                planes[(gate, kind)] = keep.tile([P, HIDDEN], U8, name="planes%d%d" % (gate, kind), align_bytes=64)
-                nc.vector.memset(planes[(gate, kind)][:].bitcast(I32), 0)
+        for slab in slabs:
+            planes[slab] = keep.tile([P, HIDDEN], U8, name="planes%d%d%d" % slab, align_bytes=64)
+            nc.vector.memset(planes[slab][:].bitcast(I32), 0)
 
         ident_f32 = keep.tile([P, P], F32)
         make_identity(nc, ident_f32[:])
@@ -94,70 +105,97 @@ def tile_lstm_pa_e_kernel(
         x_sb = keep.tile([P, BATCH_TILES, HIDDEN], BF16)
         cell_sb = keep.tile([P, BATCH_TILES, HIDDEN], BF16)
 
-        def load_scale_planes(gate, kind):
-            by_plane = scales_in_hbm[kind].rearrange("(k s) q n -> k s q n", k=GATES)
-            for quadrant in range(4):
+        def load_scale_planes(slab, quadrants=range(4)):
+            layer, kind, g = slab
+            by_gate = scales_in_hbm[kind].rearrange("(k l g) q n -> l g k q n", k=GATES, l=LAYERS)
+            for quadrant in quadrants:
                 nc.sync.dma_start(
-                    out=planes[(gate, kind)][32 * quadrant : 32 * quadrant + 16, :].bitcast(I32),
-                    in_=by_plane[gate, :, 4 * quadrant : 4 * quadrant + 4, :].bitcast(I32),
+                    out=planes[slab][32 * quadrant : 32 * quadrant + 16, :].bitcast(I32),
+                    in_=by_gate[layer, g, :, 4 * quadrant : 4 * quadrant + 4, :].bitcast(I32),
                 )
 
         weights = {}
 
-        def load_weights(layer, gate, kind):
-            w = weight_pool.tile([P, K_PASSES, HIDDEN], I32, name="w", tag="w", align_bytes=64)
-            first = (gate * LAYERS + layer) * K_PASSES
-            source = words_in_hbm[kind][first : first + K_PASSES].rearrange("g p n t -> p g (n t)").bitcast(I32)
-            nc.sync.dma_start(out=w[:], in_=source)
-            weights[(layer, gate, kind)] = w
+        def load_pass(layer, gate, kind, g):
+            group = (gate * LAYERS + layer) * K_PASSES + g
+            w = weight_pool.tile([P, HIDDEN], I32, name="w", tag="w", align_bytes=64)
+            nc.sync.dma_start(out=w[:], in_=words_in_hbm[kind][group].rearrange("p n t -> p (n t)").bitcast(I32))
+            for h in BOTH:
+                weights[(layer, gate, kind, g, h)] = w[:, columns(h)]
+
+        def load_half(layer, gate, kind, h):
+            group = (gate * LAYERS + layer) * K_PASSES
+            w = weight_pool.tile([P, K_PASSES, HALF], I32, name="w", tag="w", align_bytes=64)
+            source = words_in_hbm[kind][group : group + K_PASSES].rearrange("g p n t -> p g (n t)").bitcast(I32)
+            nc.sync.dma_start(out=w[:], in_=source[:, :, columns(h)])
+            for g in range(K_PASSES):
+                weights[(layer, gate, kind, g, h)] = w[:, g, :]
+
+        def load_step(step, kind):
+            layer, gate, hs = step
+            if hs == BOTH:
+                for g in range(K_PASSES):
+                    load_pass(layer, gate, kind, g)
+            else:
+                load_half(layer, gate, kind, hs[0])
 
         nc.sync.dma_start(out=hidden_sb[:], in_=by_partition(hidden))
-        for gate in GATE_ORDER:
+        for kind in (HH, IH):
+            if kind == IH:
+                nc.sync.dma_start(out=x_sb[:], in_=by_partition(x))
+            for g in range(K_PASSES):
+                load_scale_planes((0, kind, g))
+                load_pass(0, GATE_F, kind, g)
+        small = [(slab, (quadrant,)) for slab in slabs if slab[0] == 1 for quadrant in range(4)]
+        for step in STEPS[1:6]:
             for kind in (HH, IH):
-                load_scale_planes(gate, kind)
-                load_weights(0, gate, kind)
-                if gate == GATE_ORDER[0] and kind == HH:
-                    nc.sync.dma_start(out=x_sb[:], in_=by_partition(x))
-            if gate == GATE_ORDER[0]:
-                nc.sync.dma_start(out=cell_sb[:], in_=by_partition(cell_state))
+                load_step(step, kind)
+                if step == STEPS[1]:
+                    if kind == HH:
+                        nc.sync.dma_start(out=cell_sb[:], in_=by_partition(cell_state))
+                    continue
+                for slab, quadrants in small[0:3]:
+                    load_scale_planes(slab, quadrants)
+                small = small[3:]
 
         bias_all = keep.tile([P, n_bias_rows, HALF], F32)
 
         def bias_row(layer, gate, h):
             return (gate * LAYERS + layer) * HALVES + h
 
-        def spread_bias(layer):
-            for gate in GATE_ORDER:
-                for h in range(HALVES):
-                    r = bias_row(layer, gate, h)
-                    bias_bank = sums.tile([P, HALF], F32, tag="sum")
-                    nc.tensor.matmul(
-                        out=bias_bank[:],
-                        lhsT=bias_pick[:, r : r + 1].to_broadcast([P, P]),
-                        rhs=bias_rows[:],
-                        start=True,
-                        stop=True,
-                    )
-                    if h == 0:
-                        nc.scalar.copy(out=bias_all[:, r, :], in_=bias_bank[:])
-                    else:
-                        nc.vector.tensor_copy(out=bias_all[:, r, :], in_=bias_bank[:])
+        def spread_bias(layer, gate, copies):
+            for h in range(HALVES):
+                r = bias_row(layer, gate, h)
+                bias_bank = psum.tile([P, HALF], F32, name="bias_bank", tag="bank")
+                nc.tensor.matmul(
+                    out=bias_bank[:],
+                    lhsT=bias_pick[:, r : r + 1].to_broadcast([P, P]),
+                    rhs=bias_rows[:],
+                    start=True,
+                    stop=True,
+                )
+                copies[h](out=bias_all[:, r, :], in_=bias_bank[:])
 
         def new_mx_operand(name):
             codes = keep.tile([P, BATCH_TILES, K_PASSES, P], U32, name=name + "_codes", align_bytes=64)
             scales = keep.tile([P, BATCH_TILES, K_PASSES, P], U8, name=name + "_scales", align_bytes=64)
             return codes, scales
 
-        def quantise_input(source_sb, codes, scales):
-            for j in range(BATCH_TILES):
+        hidden_codes, hidden_scales = new_mx_operand("hidden")
+        x_codes, x_scales = new_mx_operand("x")
+        x1_codes, x1_scales = new_mx_operand("x1")
+        layer_input = {0: (x_codes, x_scales), 1: (x1_codes, x1_scales)}
+
+        def quantise_input(source_sb, codes, scales, copies):
+            for j, copy in enumerate(copies):
                 pairs = source_sb[:, j, :].bitcast(F32)
-                flipped = flips.tile([P, K_PASSES, 2, P], F32, tag="flip")
+                flipped = psum.tile([P, K_PASSES, 2, P], F32, name="flipped", tag="bank")
                 for g in range(K_PASSES):
                     for u in range(2):
                         first = (HALF // 2) * g + u
                         nc.tensor.transpose(flipped[:, g, u, :], pairs[:, first : (HALF // 2) * (g + 1) : 2], ident_f32[:])
-                grouped = stage.tile([P, K_PASSES * P * PACK], BF16, tag="grouped", align_bytes=64)
-                nc.scalar.copy(
+                grouped = stage.tile([P, K_PASSES * P * PACK], BF16, name="grouped", tag="grouped", align_bytes=64)
+                copy(
                     out=grouped[:].bitcast(F32).rearrange("p (g b u) -> p g b u", g=K_PASSES, u=2),
                     in_=flipped[:].rearrange("p g u b -> p g b u"),
                 )
@@ -167,99 +205,159 @@ def tile_lstm_pa_e_kernel(
                     in_=grouped[:],
                 )
 
-        hidden_codes, hidden_scales = new_mx_operand("hidden")
-        x_codes, x_scales = new_mx_operand("x")
-        x1_codes, x1_scales = new_mx_operand("x1")
-        layer_input = {0: (x_codes, x_scales), 1: (x1_codes, x1_scales)}
-
-        quantise_input(hidden_sb, hidden_codes, hidden_scales)
-        spread_bias(0)
-        quantise_input(x_sb, x_codes, x_scales)
-        spread_bias(1)
-
-        def mx_passes(banks, layer, gate, kind, codes, scales):
-            for g in range(K_PASSES):
-                w = weights[(layer, gate, kind)]
-                plane = 4 * (layer * K_PASSES + g)
-                for h, j in pieces:
-                    nc.tensor.matmul_mx(
-                        out=banks[(h, j)][:],
-                        lhsT=codes[:, j, g, :].bitcast(FP8X4),
-                        lhsT_scale=scales[:, j, g, :],
-                        rhs=w[:, g, columns(h)].bitcast(FP8X4),
-                        rhs_scale=planes[(gate, kind)][plane:P, columns(h)],
-                        start=(kind == HH and g == 0),
-                        stop=(kind == IH and g == K_PASSES - 1),
-                    )
-
-        def open_gate(layer, gate):
-            banks = {}
-            for h, j in pieces:
-                banks[(h, j)] = sums.tile([P, HALF], F32, name="gate_bank", tag="sum")
-            mx_passes(banks, layer, gate, HH, hidden_codes, hidden_scales)
-            return banks
-
-        def on_pieces(tile):
-            return [tile[:, j, columns(h)] for h, j in pieces]
-
-        steps = [(layer, gate) for layer in range(LAYERS) for gate in GATE_ORDER]
-        cell = {0: cell_sb}
-        acts = {}
         x1_sb = keep.tile([P, BATCH_TILES, HIDDEN], BF16)
 
-        banks = open_gate(*steps[0])
-        for n, (layer, gate) in enumerate(steps):
-            mx_passes(banks, layer, gate, IH, *layer_input[layer])
-            if layer == 0:
-                for kind in (HH, IH):
-                    load_weights(1, gate, kind)
+        def flip_x1(h):
+            flipped = []
+            for j in range(BATCH_TILES):
+                bank = psum.tile([P, PACK, P], BF16, name="flipped_x1", tag="bank")
+                for t in range(PACK):
+                    nc.tensor.transpose(bank[:, t, :], x1_sb[:, j, HALF * h + t : HALF * (h + 1) : PACK], ident_bf16[:])
+                flipped.append(bank)
+            return flipped
 
-            act = work.tile([P, BATCH_TILES, HIDDEN], F32, name="act%d" % gate, tag="act%d" % gate)
-            acts[gate] = act
-            for h, j in pieces:
-                nc.vector.tensor_tensor(
-                    out=act[:, j, columns(h)], in0=banks[(h, j)][:], in1=bias_all[:, bias_row(layer, gate, h), :], op=ADD
+        def quantise_x1(h, flipped):
+            for j in range(BATCH_TILES):
+                grouped = stage.tile([P, P, PACK], BF16, name="grouped_x1", tag="grouped_x1", align_bytes=64)
+                nc.scalar.copy(out=grouped[:], in_=flipped[j][:].rearrange("p t b -> p b t"))
+                nc.vector.quantize_mx(
+                    out=x1_codes[:, j, h, :].bitcast(FP8X4),
+                    scales=x1_scales[:, j, h, :],
+                    in_=grouped[:].rearrange("p b t -> p (b t)"),
                 )
-            if n + 1 < len(steps):
-                banks = open_gate(*steps[n + 1])
 
-            for piece in on_pieces(act):
-                nc.scalar.activation(out=piece, in_=piece, func=GATE_FUNC[gate])
+        banks = {}
+
+        def at(tile, h, j):
+            return tile[:, j, columns(h)]
+
+        def pieces(hs):
+            return [(h, j) for h in hs for j in range(BATCH_TILES)]
+
+        def passes(step, kind, codes, scales, g_outermost):
+            layer, gate, hs = step
+            order = [(h, j, g) for h, j in pieces(hs) for g in range(K_PASSES)]
+            if g_outermost:
+                order = [(h, j, g) for g in range(K_PASSES) for h, j in pieces(hs)]
+            for h, j, g in order:
+                nc.tensor.matmul_mx(
+                    out=banks[(layer, gate, h, j)][:],
+                    lhsT=codes[:, j, g, :].bitcast(FP8X4),
+                    lhsT_scale=scales[:, j, g, :],
+                    rhs=weights[(layer, gate, kind, g, h)].bitcast(FP8X4),
+                    rhs_scale=planes[(layer, kind, g)][4 * gate : P, columns(h)],
+                    start=(kind == HH and g == 0),
+                    stop=(kind == IH and g == K_PASSES - 1),
+                )
+
+        def open_step(step):
+            layer, gate, hs = step
+            for h, j in pieces(hs):
+                banks[(layer, gate, h, j)] = psum.tile([P, HALF], F32, name="gate_bank", tag="bank")
+            passes(step, HH, hidden_codes, hidden_scales, g_outermost=step == STEPS[0])
+
+        def close_step(step):
+            layer, gate, hs = step
+            codes, scales = layer_input[layer]
+            passes(step, IH, codes, scales, g_outermost=(layer, gate) == (1, GATE_F))
+
+        acts = {}
+        cell = {0: cell_sb}
+        tanh_cell = {}
+
+        def empty_step(step):
+            layer, gate, hs = step
+            if hs[0] == 0:
+                acts[(layer, gate)] = work.tile([P, BATCH_TILES, HIDDEN], F32, name="act%d" % gate, tag="act%d" % gate)
+            for h, j in pieces(hs):
+                nc.vector.tensor_tensor(
+                    out=at(acts[(layer, gate)], h, j),
+                    in0=banks[(layer, gate, h, j)][:],
+                    in1=bias_all[:, bias_row(layer, gate, h), :],
+                    op=ADD,
+                )
+
+        def apply_function(layer, gate, hs):
+            for h, j in pieces(hs):
+                z = at(acts[(layer, gate)], h, j)
+                nc.scalar.activation(out=z, in_=z, func=GATE_FUNC[gate])
+
+        def multiply_f_by_c(layer, hs):
+            for h, j in pieces(hs):
+                f = at(acts[(layer, GATE_F)], h, j)
+                nc.vector.tensor_tensor(out=f, in0=f, in1=at(cell[layer], h, j), op=MULT)
+
+        def update_cell(layer, h):
+            if h == 0:
+                cell[layer + 1] = work.tile([P, BATCH_TILES, HIDDEN], F32, name="cell", tag="cell", bufs=2)
+                tanh_cell[layer] = work.tile([P, BATCH_TILES, HIDDEN], F32, name="tanh_cell", tag="tanh_cell")
+            for j in range(BATCH_TILES):
+                i = at(acts[(layer, GATE_I)], h, j)
+                nc.vector.tensor_tensor(out=i, in0=i, in1=at(acts[(layer, GATE_G)], h, j), op=MULT)
+            for j in range(BATCH_TILES):
+                c = at(cell[layer + 1], h, j)
+                nc.vector.tensor_tensor(
+                    out=c, in0=at(acts[(layer, GATE_F)], h, j), in1=at(acts[(layer, GATE_I)], h, j), op=ADD
+                )
+            for j in range(BATCH_TILES):
+                c = at(cell[layer + 1], h, j)
+                nc.scalar.activation(out=at(tanh_cell[layer], h, j), in_=c, func=TANH)
+                if layer == LAYERS - 1:
+                    nc.sync.dma_start(out=at(by_partition(out_1), h, j), in_=c)
+
+        def multiply_o_by_tanh(layer, h):
+            for j in range(BATCH_TILES):
+                o = at(acts[(layer, GATE_O)], h, j)
+                product = o if layer == LAYERS - 1 else at(x1_sb, h, j)
+                nc.vector.tensor_tensor(out=product, in0=o, in1=at(tanh_cell[layer], h, j), op=MULT)
+                if layer == LAYERS - 1:
+                    nc.sync.dma_start(out=at(by_partition(out_0), h, j), in_=product)
+
+        on_scalar = (nc.scalar.copy, nc.scalar.copy)
+        on_both = (nc.scalar.copy, nc.vector.tensor_copy)
+        quantise_input(hidden_sb, hidden_codes, hidden_scales, on_both)
+        spread_bias(0, GATE_F, on_both)
+        spread_bias(0, GATE_I, on_both)
+        open_step(STEPS[0])
+        quantise_input(x_sb, x_codes, x_scales, on_both)
+        spread_bias(0, GATE_G, (nc.vector.tensor_copy, nc.scalar.copy))
+        spread_bias(0, GATE_O, on_both)
+        spread_bias(1, GATE_F, on_both)
+
+        for n, step in enumerate(STEPS):
+            layer, gate, hs = step
+            close_step(step)
+            empty_step(step)
+            if n + 1 == len(STEPS):
+                multiply_o_by_tanh(layer, 0)
+            else:
+                open_step(STEPS[n + 1])
 
             if gate == GATE_F:
-                for f, c in zip(on_pieces(act), on_pieces(cell[layer])):
-                    nc.vector.tensor_tensor(out=f, in0=f, in1=c, op=MULT)
+                apply_function(layer, gate, hs)
+                if layer == 0:
+                    spread_bias(1, GATE_I, on_scalar)
+                multiply_f_by_c(layer, hs)
+            if gate == GATE_I:
+                apply_function(layer, gate, hs)
+                if layer == 0:
+                    spread_bias(1, GATE_G, on_scalar)
+                    for later in STEPS[6:]:
+                        for kind in (HH, IH):
+                            load_step(later, kind)
             if gate == GATE_G:
-                new_cell = work.tile([P, BATCH_TILES, HIDDEN], F32, name="cell", tag="cell", bufs=2)
-                cell[layer + 1] = new_cell
-                tanh_cell = work.tile([P, BATCH_TILES, HIDDEN], F32, name="tanh_cell", tag="tanh_cell")
-                for i, g_act in zip(on_pieces(acts[GATE_I]), on_pieces(act)):
-                    nc.vector.tensor_tensor(out=i, in0=i, in1=g_act, op=MULT)
-                for c, fc, ig in zip(on_pieces(new_cell), on_pieces(acts[GATE_F]), on_pieces(acts[GATE_I])):
-                    nc.vector.tensor_tensor(out=c, in0=fc, in1=ig, op=ADD)
-                for t, c in zip(on_pieces(tanh_cell), on_pieces(new_cell)):
-                    nc.scalar.activation(out=t, in_=c, func=TANH)
-                if layer == LAYERS - 1:
-                    for c_hbm, c in zip(on_pieces(by_partition(out_1)), on_pieces(new_cell)):
-                        nc.sync.dma_start(out=c_hbm, in_=c)
+                apply_function(layer, gate, hs)
+                for h in hs:
+                    update_cell(layer, h)
+                if layer == 0:
+                    spread_bias(1, GATE_O, on_scalar)
             if gate == GATE_O and layer == 0:
-                for x1, o, t in zip(on_pieces(x1_sb), on_pieces(act), on_pieces(tanh_cell)):
-                    nc.vector.tensor_tensor(out=x1, in0=o, in1=t, op=MULT)
-                grouped_x1 = {}
-                for g, j in pieces:
-                    flipped = flips.tile([P, PACK, P], BF16, tag="flip")
-                    for t in range(PACK):
-                        nc.tensor.transpose(flipped[:, t, :], x1_sb[:, j, HALF * g + t : HALF * (g + 1) : PACK], ident_bf16[:])
-                    grouped = stage.tile([P, P, PACK], BF16, tag="grouped_x1", bufs=len(pieces), align_bytes=64)
-                    nc.scalar.copy(out=grouped[:], in_=flipped[:].rearrange("p t b -> p b t"))
-                    grouped_x1[(g, j)] = grouped
-                for g, j in pieces:
-                    nc.vector.quantize_mx(
-                        out=x1_codes[:, j, g, :].bitcast(FP8X4),
-                        scales=x1_scales[:, j, g, :],
-                        in_=grouped_x1[(g, j)][:].rearrange("p b t -> p (b t)"),
-                    )
+                for h in hs:
+                    apply_function(layer, gate, (h,))
+                    multiply_o_by_tanh(layer, h)
+                for h in hs:
+                    quantise_x1(h, flip_x1(h))
             if gate == GATE_O and layer == LAYERS - 1:
-                for x2_hbm, o, t in zip(on_pieces(by_partition(out_0)), on_pieces(act), on_pieces(tanh_cell)):
-                    nc.vector.tensor_tensor(out=o, in0=o, in1=t, op=MULT)
-                    nc.sync.dma_start(out=x2_hbm, in_=o)
+                apply_function(layer, gate, hs)
+                if hs == (1,):
+                    multiply_o_by_tanh(layer, 1)

@@ -282,10 +282,10 @@ def tile_lstm_pa_e_kernel(
                 z = at(acts[(layer, gate)], h, j)
                 nc.scalar.activation(out=z, in_=z, func=GATE_FUNC[gate])
 
-        def multiply_f_by_c(layer, hs):
+        def multiply_f_by_c(layer, hs, eng):
             for h, j in pieces(hs):
                 f = at(acts[(layer, GATE_F)], h, j)
-                nc.vector.tensor_tensor(out=f, in0=f, in1=at(cell[layer], h, j), op=MULT)
+                eng.tensor_tensor(out=f, in0=f, in1=at(cell[layer], h, j), op=MULT)
 
         def update_cell(layer, h):
             if h == 0:
@@ -337,7 +337,7 @@ def tile_lstm_pa_e_kernel(
                 apply_function(layer, gate, hs)
                 if layer == 0:
                     spread_bias(1, GATE_I, on_scalar)
-                multiply_f_by_c(layer, hs)
+                multiply_f_by_c(layer, hs, nc.gpsimd if layer == 1 else nc.vector)
             if gate == GATE_I:
                 apply_function(layer, gate, hs)
                 if layer == 0:

@@ -105,10 +105,10 @@ def tile_lstm_pa_e_kernel(
         x_sb = keep.tile([P, BATCH_TILES, HIDDEN], BF16)
         cell_sb = keep.tile([P, BATCH_TILES, HIDDEN], BF16)
 
-        def load_scale_planes(slab, quadrants=range(4)):
+        def load_scale_planes(slab):
             layer, kind, g = slab
             by_gate = scales_in_hbm[kind].rearrange("(k l g) q n -> l g k q n", k=GATES, l=LAYERS)
-            for quadrant in quadrants:
+            for quadrant in range(4):
                 nc.sync.dma_start(
                     out=planes[slab][32 * quadrant : 32 * quadrant + 16, :].bitcast(I32),
                     in_=by_gate[layer, g, :, 4 * quadrant : 4 * quadrant + 4, :].bitcast(I32),
@@ -146,17 +146,15 @@ def tile_lstm_pa_e_kernel(
             for g in range(K_PASSES):
                 load_scale_planes((0, kind, g))
                 load_pass(0, GATE_F, kind, g)
-        small = [(slab, (quadrant,)) for slab in slabs if slab[0] == 1 for quadrant in range(4)]
+        later_slabs = [slab for slab in slabs if slab[0] == 1]
         for step in STEPS[1:6]:
             for kind in (HH, IH):
                 load_step(step, kind)
-                if step == STEPS[1]:
-                    if kind == HH:
-                        nc.sync.dma_start(out=cell_sb[:], in_=by_partition(cell_state))
-                    continue
-                for slab, quadrants in small[0:3]:
-                    load_scale_planes(slab, quadrants)
-                small = small[3:]
+                if step == STEPS[1] and kind == HH:
+                    nc.sync.dma_start(out=cell_sb[:], in_=by_partition(cell_state))
+                if step in STEPS[3:5]:
+                    load_scale_planes(later_slabs[0])
+                    later_slabs = later_slabs[1:]
 
         bias_all = keep.tile([P, n_bias_rows, HALF], F32)
 
@@ -265,11 +263,11 @@ def tile_lstm_pa_e_kernel(
         cell = {0: cell_sb}
         tanh_cell = {}
 
-        def empty_step(step):
+        def empty_step(step, js=(0, 1)):
             layer, gate, hs = step
             if hs[0] == 0:
                 acts[(layer, gate)] = work.tile([P, BATCH_TILES, HIDDEN], F32, name="act%d" % gate, tag="act%d" % gate)
-            for h, j in pieces(hs):
+            for h, j in [(h, j) for h, j in pieces(hs) if j in js]:
                 nc.vector.tensor_tensor(
                     out=at(acts[(layer, gate)], h, j),
                     in0=banks[(layer, gate, h, j)][:],
@@ -305,8 +303,8 @@ def tile_lstm_pa_e_kernel(
                 if layer == LAYERS - 1:
                     nc.sync.dma_start(out=at(by_partition(out_1), h, j), in_=c)
 
-        def multiply_o_by_tanh(layer, h):
-            for j in range(BATCH_TILES):
+        def multiply_o_by_tanh(layer, h, js=(0, 1)):
+            for j in js:
                 o = at(acts[(layer, GATE_O)], h, j)
                 product = o if layer == LAYERS - 1 else at(x1_sb, h, j)
                 nc.vector.tensor_tensor(out=product, in0=o, in1=at(tanh_cell[layer], h, j), op=MULT)
@@ -323,25 +321,28 @@ def tile_lstm_pa_e_kernel(
         spread_bias(0, GATE_G, (nc.vector.tensor_copy, nc.scalar.copy))
         spread_bias(0, GATE_O, on_both)
         spread_bias(1, GATE_F, on_both)
+        spread_bias(1, GATE_I, on_scalar)
 
         for n, step in enumerate(STEPS):
             layer, gate, hs = step
             close_step(step)
-            empty_step(step)
             if n + 1 == len(STEPS):
-                multiply_o_by_tanh(layer, 0)
+                for j in range(BATCH_TILES):
+                    empty_step(step, (j,))
+                    multiply_o_by_tanh(layer, 0, (j,))
             else:
+                empty_step(step)
                 open_step(STEPS[n + 1])
 
             if gate == GATE_F:
                 apply_function(layer, gate, hs)
                 if layer == 0:
-                    spread_bias(1, GATE_I, on_scalar)
+                    spread_bias(1, GATE_G, on_scalar)
+                    spread_bias(1, GATE_O, on_scalar)
                 multiply_f_by_c(layer, hs, nc.gpsimd if layer == 1 else nc.vector)
             if gate == GATE_I:
                 apply_function(layer, gate, hs)
                 if layer == 0:
-                    spread_bias(1, GATE_G, on_scalar)
                     for later in STEPS[6:]:
                         for kind in (HH, IH):
                             load_step(later, kind)
@@ -349,8 +350,6 @@ def tile_lstm_pa_e_kernel(
                 apply_function(layer, gate, hs)
                 for h in hs:
                     update_cell(layer, h)
-                if layer == 0:
-                    spread_bias(1, GATE_O, on_scalar)
             if gate == GATE_O and layer == 0:
                 for h in hs:
                     apply_function(layer, gate, (h,))

@@ -147,14 +147,15 @@ def tile_lstm_pa_e_kernel(
                 load_scale_planes((0, kind, g))
                 load_pass(0, GATE_F, kind, g)
         later_slabs = [slab for slab in slabs if slab[0] == 1]
-        for step in STEPS[1:6]:
-            for kind in (HH, IH):
-                load_step(step, kind)
-                if step == STEPS[1] and kind == HH:
-                    nc.sync.dma_start(out=cell_sb[:], in_=by_partition(cell_state))
-                if step in STEPS[3:5]:
-                    load_scale_planes(later_slabs[0])
-                    later_slabs = later_slabs[1:]
+        order = [(step, kind) for step in STEPS[1:4] for kind in (HH, IH)]
+        order += [(step, kind) for kind in (HH, IH) for step in STEPS[4:6]]
+        for step, kind in order:
+            load_step(step, kind)
+            if step == STEPS[1] and kind == HH:
+                nc.sync.dma_start(out=cell_sb[:], in_=by_partition(cell_state))
+            if step in STEPS[3:5]:
+                load_scale_planes(later_slabs[0])
+                later_slabs = later_slabs[1:]
 
         bias_all = keep.tile([P, n_bias_rows, HALF], F32)
 
@@ -185,22 +186,25 @@ def tile_lstm_pa_e_kernel(
         layer_input = {0: (x_codes, x_scales), 1: (x1_codes, x1_scales)}
 
         def quantise_input(source_sb, codes, scales, copies):
-            for j, copy in enumerate(copies):
+            grouped = []
+            for j in range(BATCH_TILES):
                 pairs = source_sb[:, j, :].bitcast(F32)
                 flipped = psum.tile([P, K_PASSES, 2, P], F32, name="flipped", tag="bank")
                 for g in range(K_PASSES):
                     for u in range(2):
                         first = (HALF // 2) * g + u
                         nc.tensor.transpose(flipped[:, g, u, :], pairs[:, first : (HALF // 2) * (g + 1) : 2], ident_f32[:])
-                grouped = stage.tile([P, K_PASSES * P * PACK], BF16, name="grouped", tag="grouped", align_bytes=64)
-                copy(
-                    out=grouped[:].bitcast(F32).rearrange("p (g b u) -> p g b u", g=K_PASSES, u=2),
+                words = stage.tile([P, K_PASSES * P * PACK], BF16, name="grouped", tag="grouped", align_bytes=64)
+                copies[j](
+                    out=words[:].bitcast(F32).rearrange("p (g b u) -> p g b u", g=K_PASSES, u=2),
                     in_=flipped[:].rearrange("p g u b -> p g b u"),
                 )
+                grouped.append(words)
+            for j in range(BATCH_TILES):
                 nc.vector.quantize_mx(
                     out=codes[:, j].rearrange("p g b -> p (g b)").bitcast(FP8X4),
                     scales=scales[:, j].rearrange("p g b -> p (g b)"),
-                    in_=grouped[:],
+                    in_=grouped[j][:],
                 )
 
         x1_sb = keep.tile([P, BATCH_TILES, HIDDEN], BF16)
@@ -314,14 +318,12 @@ def tile_lstm_pa_e_kernel(
         on_scalar = (nc.scalar.copy, nc.scalar.copy)
         on_both = (nc.scalar.copy, nc.vector.tensor_copy)
         quantise_input(hidden_sb, hidden_codes, hidden_scales, on_both)
-        spread_bias(0, GATE_F, on_both)
-        spread_bias(0, GATE_I, on_both)
+        spread_bias(0, GATE_F, (nc.scalar.copy, nc.vector.tensor_copy))
+        spread_bias(0, GATE_I, (nc.scalar.copy, nc.vector.tensor_copy))
         open_step(STEPS[0])
         quantise_input(x_sb, x_codes, x_scales, on_both)
         spread_bias(0, GATE_G, (nc.vector.tensor_copy, nc.scalar.copy))
-        spread_bias(0, GATE_O, on_both)
-        spread_bias(1, GATE_F, on_both)
-        spread_bias(1, GATE_I, on_scalar)
+        spread_bias(0, GATE_O, (nc.scalar.copy, nc.vector.tensor_copy))
 
         for n, step in enumerate(STEPS):
             layer, gate, hs = step
@@ -332,17 +334,20 @@ def tile_lstm_pa_e_kernel(
                     multiply_o_by_tanh(layer, 0, (j,))
             else:
                 empty_step(step)
-                open_step(STEPS[n + 1])
+                if step != STEPS[4]:
+                    open_step(STEPS[n + 1])
 
             if gate == GATE_F:
                 apply_function(layer, gate, hs)
                 if layer == 0:
-                    spread_bias(1, GATE_G, on_scalar)
-                    spread_bias(1, GATE_O, on_scalar)
+                    spread_bias(1, GATE_F, (nc.scalar.copy, nc.scalar.copy))
+                    spread_bias(1, GATE_I, (nc.scalar.copy, nc.scalar.copy))
                 multiply_f_by_c(layer, hs, nc.gpsimd if layer == 1 else nc.vector)
             if gate == GATE_I:
                 apply_function(layer, gate, hs)
                 if layer == 0:
+                    spread_bias(1, GATE_G, (nc.vector.tensor_copy, nc.vector.tensor_copy))
+                    spread_bias(1, GATE_O, (nc.scalar.copy, nc.scalar.copy))
                     for later in STEPS[6:]:
                         for kind in (HH, IH):
                             load_step(later, kind)
@@ -354,8 +359,9 @@ def tile_lstm_pa_e_kernel(
                 for h in hs:
                     apply_function(layer, gate, (h,))
                     multiply_o_by_tanh(layer, h)
-                for h in hs:
-                    quantise_x1(h, flip_x1(h))
+                open_step(STEPS[n + 2])
+                quantise_x1(0, flip_x1(0))
+                quantise_x1(1, flip_x1(1))
             if gate == GATE_O and layer == LAYERS - 1:
                 apply_function(layer, gate, hs)
                 if hs == (1,):

@@ -289,7 +289,7 @@ def tile_lstm_pa_e_kernel(
                 f = at(acts[(layer, GATE_F)], h, j)
                 eng.tensor_tensor(out=f, in0=f, in1=at(cell[layer], h, j), op=MULT)
 
-        def update_cell(layer, h):
+        def update_cell(layer, h, add_on):
             if h == 0:
                 cell[layer + 1] = work.tile([P, BATCH_TILES, HIDDEN], F32, name="cell", tag="cell", bufs=2)
                 tanh_cell[layer] = work.tile([P, BATCH_TILES, HIDDEN], F32, name="tanh_cell", tag="tanh_cell")
@@ -298,9 +298,11 @@ def tile_lstm_pa_e_kernel(
                 nc.vector.tensor_tensor(out=i, in0=i, in1=at(acts[(layer, GATE_G)], h, j), op=MULT)
             for j in range(BATCH_TILES):
                 c = at(cell[layer + 1], h, j)
-                nc.vector.tensor_tensor(
+                add_on.tensor_tensor(
                     out=c, in0=at(acts[(layer, GATE_F)], h, j), in1=at(acts[(layer, GATE_I)], h, j), op=ADD
                 )
+
+        def tanh_of_cell(layer, h):
             for j in range(BATCH_TILES):
                 c = at(cell[layer + 1], h, j)
                 nc.scalar.activation(out=at(tanh_cell[layer], h, j), in_=c, func=TANH)
@@ -354,7 +356,13 @@ def tile_lstm_pa_e_kernel(
             if gate == GATE_G:
                 apply_function(layer, gate, hs)
                 for h in hs:
-                    update_cell(layer, h)
+                    if (layer, h) == (1, 0):
+                        update_cell(layer, h, nc.gpsimd)
+                        continue
+                    if layer == 1:
+                        tanh_of_cell(layer, 0)
+                    update_cell(layer, h, nc.vector)
+                    tanh_of_cell(layer, h)
             if gate == GATE_O and layer == 0:
                 for h in hs:
                     apply_function(layer, gate, (h,))

from contextlib import ExitStack

import concourse.mybir as mybir
from concourse.masks import make_identity

F32 = mybir.dt.float32
BF16 = mybir.dt.bfloat16
I32 = mybir.dt.int32
U32 = mybir.dt.uint32
U8 = mybir.dt.uint8
FP8X4 = mybir.dt.float8_e4m3fn_x4
SIGMOID = mybir.ActivationFunctionType.Sigmoid
TANH = mybir.ActivationFunctionType.Tanh
ADD = mybir.AluOpType.add
MULT = mybir.AluOpType.mult

P = 128
PACK = 4
BATCH = 256
HIDDEN = 1024
LAYERS = 2
GATES = 4
BATCH_TILES = BATCH // P
K_PASSES = HIDDEN // (P * PACK)
HALF = 512
HALVES = HIDDEN // HALF

GATE_I = 0
GATE_F = 1
GATE_G = 2
GATE_O = 3
BOTH = (0, 1)
STEPS = (
    (0, GATE_F, BOTH),
    (0, GATE_I, BOTH),
    (0, GATE_G, BOTH),
    (0, GATE_O, BOTH),
    (1, GATE_F, BOTH),
    (1, GATE_I, (0,)),
    (1, GATE_G, (0,)),
    (1, GATE_I, (1,)),
    (1, GATE_G, (1,)),
    (1, GATE_O, (0,)),
    (1, GATE_O, (1,)),
)
GATE_FUNC = {GATE_I: SIGMOID, GATE_F: SIGMOID, GATE_G: TANH, GATE_O: SIGMOID}

HH = 0
IH = 1

FLOPS = 2 * LAYERS * GATES * 2 * BATCH * HIDDEN * HIDDEN


def tile_lstm_pa_e_kernel(
    tc, x, hidden, cell_state, w_ih_words, w_ih_scales, w_hh_words, w_hh_scales, b_ih, b_hh, out_0, out_1
):
    nc = tc.nc
    words_in_hbm = {HH: w_hh_words, IH: w_ih_words}
    scales_in_hbm = {HH: w_hh_scales, IH: w_ih_scales}

    def by_partition(array):
        return array.rearrange("(p j) n -> p j n", j=BATCH_TILES)

    def columns(h):
        return slice(h * HALF, (h + 1) * HALF)

    with ExitStack() as stack:
        stack.enter_context(tc.manual_schedule())
        keep = stack.enter_context(tc.tile_pool(name="keep", bufs=1))
        weight_pool = stack.enter_context(tc.tile_pool(name="weights", bufs=24))
        stage = stack.enter_context(tc.tile_pool(name="stage", bufs=2))
        work = stack.enter_context(tc.tile_pool(name="work", bufs=1))
        psum = stack.enter_context(tc.psum_pool(name="psum", bufs=8))

        bias_rows = keep.tile([P, HALF], BF16)
        n_bias_rows = GATES * LAYERS * HALVES
        nc.gpsimd.memset(bias_rows[:], 0.0)
        nc.scalar.dma_start(out=bias_rows[0:n_bias_rows, :], in_=b_ih.rearrange("k l (h n) -> (k l h) n", h=HALVES))
        nc.scalar.dma_start(
            out=bias_rows[n_bias_rows : 2 * n_bias_rows, :], in_=b_hh.rearrange("k l (h n) -> (k l h) n", h=HALVES)
        )

        slabs = [(layer, kind, g) for layer in range(LAYERS) for kind in (HH, IH) for g in range(K_PASSES)]
        planes = {}
        for slab in slabs:
            planes[slab] = keep.tile([P, HIDDEN], U8, name="planes%d%d%d" % slab, align_bytes=64)
            nc.vector.memset(planes[slab][:].bitcast(I32), 0)

        ident_f32 = keep.tile([P, P], F32)
        make_identity(nc, ident_f32[:])
        ident_bf16 = keep.tile([P, P], BF16)
        make_identity(nc, ident_bf16[:])
        bias_pick = keep.tile([P, n_bias_rows], BF16)
        nc.vector.tensor_tensor(
            out=bias_pick[:],
            in0=ident_bf16[:, 0:n_bias_rows],
            in1=ident_bf16[:, n_bias_rows : 2 * n_bias_rows],
            op=ADD,
        )
        table_warmer = keep.tile([P, 1], F32)
        nc.vector.memset(table_warmer[:], 0.0)
        nc.scalar.activation(out=table_warmer[:], in_=table_warmer[:], func=SIGMOID)

        hidden_sb = keep.tile([P, BATCH_TILES, HIDDEN], BF16)
        x_sb = keep.tile([P, BATCH_TILES, HIDDEN], BF16)
        cell_sb = keep.tile([P, BATCH_TILES, HIDDEN], BF16)

        def load_scale_planes(slab):
            layer, kind, g = slab
            by_gate = scales_in_hbm[kind].rearrange("(k l g) q n -> l g k q n", k=GATES, l=LAYERS)
            for quadrant in range(4):
                nc.sync.dma_start(
                    out=planes[slab][32 * quadrant : 32 * quadrant + 16, :].bitcast(I32),
                    in_=by_gate[layer, g, :, 4 * quadrant : 4 * quadrant + 4, :].bitcast(I32),
                )

        weights = {}

        def load_pass(layer, gate, kind, g):
            group = (gate * LAYERS + layer) * K_PASSES + g
            w = weight_pool.tile([P, HIDDEN], I32, name="w", tag="w", align_bytes=64)
            nc.sync.dma_start(out=w[:], in_=words_in_hbm[kind][group].rearrange("p n t -> p (n t)").bitcast(I32))
            for h in BOTH:
                weights[(layer, gate, kind, g, h)] = w[:, columns(h)]

        def load_half(layer, gate, kind, h):
            group = (gate * LAYERS + layer) * K_PASSES
            w = weight_pool.tile([P, K_PASSES, HALF], I32, name="w", tag="w", align_bytes=64)
            source = words_in_hbm[kind][group : group + K_PASSES].rearrange("g p n t -> p g (n t)").bitcast(I32)
            nc.sync.dma_start(out=w[:], in_=source[:, :, columns(h)])
            for g in range(K_PASSES):
                weights[(layer, gate, kind, g, h)] = w[:, g, :]

        def load_step(step, kind):
            layer, gate, hs = step
            if hs == BOTH:
                for g in range(K_PASSES):
                    load_pass(layer, gate, kind, g)
            else:
                load_half(layer, gate, kind, hs[0])

        nc.sync.dma_start(out=hidden_sb[:], in_=by_partition(hidden))
        for kind in (HH, IH):
            if kind == IH:
                nc.sync.dma_start(out=x_sb[:], in_=by_partition(x))
            for g in range(K_PASSES):
                load_scale_planes((0, kind, g))
                load_pass(0, GATE_F, kind, g)
        later_slabs = [slab for slab in slabs if slab[0] == 1]
        order = [(step, kind) for step in STEPS[1:4] for kind in (HH, IH)]
        order += [(step, kind) for kind in (HH, IH) for step in STEPS[4:6]]
        for step, kind in order:
            load_step(step, kind)
            if step == STEPS[1] and kind == HH:
                nc.sync.dma_start(out=cell_sb[:], in_=by_partition(cell_state))
            if step in STEPS[3:5]:
                load_scale_planes(later_slabs[0])
                later_slabs = later_slabs[1:]

        bias_all = keep.tile([P, n_bias_rows, HALF], F32)

        def bias_row(layer, gate, h):
            return (gate * LAYERS + layer) * HALVES + h

        def spread_bias(layer, gate, copies):
            for h in range(HALVES):
                r = bias_row(layer, gate, h)
                bias_bank = psum.tile([P, HALF], F32, name="bias_bank", tag="bank")
                nc.tensor.matmul(
                    out=bias_bank[:],
                    lhsT=bias_pick[:, r : r + 1].to_broadcast([P, P]),
                    rhs=bias_rows[:],
                    start=True,
                    stop=True,
                )
                copies[h](out=bias_all[:, r, :], in_=bias_bank[:])

        def new_mx_operand(name):
            codes = keep.tile([P, BATCH_TILES, K_PASSES, P], U32, name=name + "_codes", align_bytes=64)
            scales = keep.tile([P, BATCH_TILES, K_PASSES, P], U8, name=name + "_scales", align_bytes=64)
            return codes, scales

        hidden_codes, hidden_scales = new_mx_operand("hidden")
        x_codes, x_scales = new_mx_operand("x")
        x1_codes, x1_scales = new_mx_operand("x1")
        layer_input = {0: (x_codes, x_scales), 1: (x1_codes, x1_scales)}

        def quantise_input(source_sb, codes, scales, copies):
            grouped = []
            for j in range(BATCH_TILES):
                pairs = source_sb[:, j, :].bitcast(F32)
                flipped = psum.tile([P, K_PASSES, 2, P], F32, name="flipped", tag="bank")
                for g in range(K_PASSES):
                    for u in range(2):
                        first = (HALF // 2) * g + u
                        nc.tensor.transpose(flipped[:, g, u, :], pairs[:, first : (HALF // 2) * (g + 1) : 2], ident_f32[:])
                words = stage.tile([P, K_PASSES * P * PACK], BF16, name="grouped", tag="grouped", align_bytes=64)
                copies[j](
                    out=words[:].bitcast(F32).rearrange("p (g b u) -> p g b u", g=K_PASSES, u=2),
                    in_=flipped[:].rearrange("p g u b -> p g b u"),
                )
                grouped.append(words)
            for j in range(BATCH_TILES):
                nc.vector.quantize_mx(
                    out=codes[:, j].rearrange("p g b -> p (g b)").bitcast(FP8X4),
                    scales=scales[:, j].rearrange("p g b -> p (g b)"),
                    in_=grouped[j][:],
                )

        x1_sb = keep.tile([P, BATCH_TILES, HIDDEN], BF16)

        def flip_x1(h):
            flipped = []
            for j in range(BATCH_TILES):
                bank = psum.tile([P, PACK, P], BF16, name="flipped_x1", tag="bank")
                for t in range(PACK):
                    nc.tensor.transpose(bank[:, t, :], x1_sb[:, j, HALF * h + t : HALF * (h + 1) : PACK], ident_bf16[:])
                flipped.append(bank)
            return flipped

        def quantise_x1(h, flipped):
            for j in range(BATCH_TILES):
                grouped = stage.tile([P, P, PACK], BF16, name="grouped_x1", tag="grouped_x1", align_bytes=64)
                nc.scalar.copy(out=grouped[:], in_=flipped[j][:].rearrange("p t b -> p b t"))
                nc.vector.quantize_mx(
                    out=x1_codes[:, j, h, :].bitcast(FP8X4),
                    scales=x1_scales[:, j, h, :],
                    in_=grouped[:].rearrange("p b t -> p (b t)"),
                )

        banks = {}

        def at(tile, h, j):
            return tile[:, j, columns(h)]

        def pieces(hs):
            return [(h, j) for h in hs for j in range(BATCH_TILES)]

        def passes(step, kind, codes, scales, g_outermost):
            layer, gate, hs = step
            order = [(h, j, g) for h, j in pieces(hs) for g in range(K_PASSES)]
            if g_outermost:
                order = [(h, j, g) for g in range(K_PASSES) for h, j in pieces(hs)]
            for h, j, g in order:
                nc.tensor.matmul_mx(
                    out=banks[(layer, gate, h, j)][:],
                    lhsT=codes[:, j, g, :].bitcast(FP8X4),
                    lhsT_scale=scales[:, j, g, :],
                    rhs=weights[(layer, gate, kind, g, h)].bitcast(FP8X4),
                    rhs_scale=planes[(layer, kind, g)][4 * gate : P, columns(h)],
                    start=(kind == HH and g == 0),
                    stop=(kind == IH and g == K_PASSES - 1),
                )

        def open_step(step):
            layer, gate, hs = step
            for h, j in pieces(hs):
                banks[(layer, gate, h, j)] = psum.tile([P, HALF], F32, name="gate_bank", tag="bank")
            passes(step, HH, hidden_codes, hidden_scales, g_outermost=step == STEPS[0])

        def close_step(step):
            layer, gate, hs = step
            codes, scales = layer_input[layer]
            passes(step, IH, codes, scales, g_outermost=(layer, gate) == (1, GATE_F))

        acts = {}
        cell = {0: cell_sb}
        tanh_cell = {}

        def empty_step(step, js=(0, 1)):
            layer, gate, hs = step
            if hs[0] == 0:
                acts[(layer, gate)] = work.tile([P, BATCH_TILES, HIDDEN], F32, name="act%d" % gate, tag="act%d" % gate)
            for h, j in [(h, j) for h, j in pieces(hs) if j in js]:
                nc.vector.tensor_tensor(
                    out=at(acts[(layer, gate)], h, j),
                    in0=banks[(layer, gate, h, j)][:],
                    in1=bias_all[:, bias_row(layer, gate, h), :],
                    op=ADD,
                )

        def apply_function(layer, gate, hs):
            for h, j in pieces(hs):
                z = at(acts[(layer, gate)], h, j)
                nc.scalar.activation(out=z, in_=z, func=GATE_FUNC[gate])

        def multiply_f_by_c(layer, hs, eng):
            for h, j in pieces(hs):
                f = at(acts[(layer, GATE_F)], h, j)
                eng.tensor_tensor(out=f, in0=f, in1=at(cell[layer], h, j), op=MULT)

        def update_cell(layer, h, add_on):
            if h == 0:
                cell[layer + 1] = work.tile([P, BATCH_TILES, HIDDEN], F32, name="cell", tag="cell", bufs=2)
                tanh_cell[layer] = work.tile([P, BATCH_TILES, HIDDEN], F32, name="tanh_cell", tag="tanh_cell")
            for j in range(BATCH_TILES):
                i = at(acts[(layer, GATE_I)], h, j)
                nc.vector.tensor_tensor(out=i, in0=i, in1=at(acts[(layer, GATE_G)], h, j), op=MULT)
            for j in range(BATCH_TILES):
                c = at(cell[layer + 1], h, j)
                add_on.tensor_tensor(
                    out=c, in0=at(acts[(layer, GATE_F)], h, j), in1=at(acts[(layer, GATE_I)], h, j), op=ADD
                )

        def tanh_of_cell(layer, h):
            for j in range(BATCH_TILES):
                c = at(cell[layer + 1], h, j)
                nc.scalar.activation(out=at(tanh_cell[layer], h, j), in_=c, func=TANH)
                if layer == LAYERS - 1:
                    nc.sync.dma_start(out=at(by_partition(out_1), h, j), in_=c)

        def multiply_o_by_tanh(layer, h, js=(0, 1)):
            for j in js:
                o = at(acts[(layer, GATE_O)], h, j)
                product = o if layer == LAYERS - 1 else at(x1_sb, h, j)
                nc.vector.tensor_tensor(out=product, in0=o, in1=at(tanh_cell[layer], h, j), op=MULT)
                if layer == LAYERS - 1:
                    nc.sync.dma_start(out=at(by_partition(out_0), h, j), in_=product)

        on_scalar = (nc.scalar.copy, nc.scalar.copy)
        on_both = (nc.scalar.copy, nc.vector.tensor_copy)
        quantise_input(hidden_sb, hidden_codes, hidden_scales, on_both)
        spread_bias(0, GATE_F, (nc.scalar.copy, nc.vector.tensor_copy))
        spread_bias(0, GATE_I, (nc.scalar.copy, nc.vector.tensor_copy))
        open_step(STEPS[0])
        quantise_input(x_sb, x_codes, x_scales, on_both)
        spread_bias(0, GATE_G, (nc.vector.tensor_copy, nc.scalar.copy))
        spread_bias(0, GATE_O, (nc.scalar.copy, nc.vector.tensor_copy))

        for n, step in enumerate(STEPS):
            layer, gate, hs = step
            close_step(step)
            if n + 1 == len(STEPS):
                for j in range(BATCH_TILES):
                    empty_step(step, (j,))
                    multiply_o_by_tanh(layer, 0, (j,))
            else:
                empty_step(step)
                if step != STEPS[4]:
                    open_step(STEPS[n + 1])

            if gate == GATE_F:
                apply_function(layer, gate, hs)
                if layer == 0:
                    spread_bias(1, GATE_F, (nc.scalar.copy, nc.scalar.copy))
                    spread_bias(1, GATE_I, (nc.scalar.copy, nc.scalar.copy))
                multiply_f_by_c(layer, hs, nc.gpsimd if layer == 1 else nc.vector)
            if gate == GATE_I:
                apply_function(layer, gate, hs)
                if layer == 0:
                    spread_bias(1, GATE_G, (nc.vector.tensor_copy, nc.vector.tensor_copy))
                    spread_bias(1, GATE_O, (nc.scalar.copy, nc.scalar.copy))
                    for later in STEPS[6:]:
                        for kind in (HH, IH):
                            load_step(later, kind)
            if gate == GATE_G:
                apply_function(layer, gate, hs)
                for h in hs:
                    if (layer, h) == (1, 0):
                        update_cell(layer, h, nc.gpsimd)
                        continue
                    if layer == 1:
                        tanh_of_cell(layer, 0)
                    update_cell(layer, h, nc.vector)
                    tanh_of_cell(layer, h)
            if gate == GATE_O and layer == 0:
                for h in hs:
                    apply_function(layer, gate, (h,))
                    multiply_o_by_tanh(layer, h)
                open_step(STEPS[n + 2])
                quantise_x1(0, flip_x1(0))
                quantise_x1(1, flip_x1(1))
            if gate == GATE_O and layer == LAYERS - 1:
                apply_function(layer, gate, hs)
                if hs == (1,):
                    multiply_o_by_tanh(layer, 1)
